import numpy as np
import ml_dtypes


def mxq(x, axis, fmt="e4m3"):
    dtype, down = {"e4m3": (ml_dtypes.float8_e4m3fn, 7), "e5m2": (ml_dtypes.float8_e5m2, 14)}[fmt]
    v = np.moveaxis(np.asarray(x, np.float32).astype(ml_dtypes.bfloat16).astype(np.float64), axis, -1)
    blocks = v.reshape(v.shape[:-1] + (-1, 32))
    amax = np.abs(blocks).max(-1, keepdims=True)
    byte = np.maximum(np.where(amax > 0, np.frexp(amax)[1] - 1 + 127, 0) - down, 1)
    scale = np.exp2(byte - 127.0)
    codes = (blocks / scale).astype(np.float32).astype(dtype).astype(np.float64)
    return np.moveaxis((codes * scale).reshape(v.shape), -1, axis)


WIDE = False


def mx_kscale(k):
    if not WIDE:
        return np.ones(k)
    levels = np.array([10, -10, 5, -5, 0])
    a = np.random.permutation(np.resize(levels, k // 512 * 4)).reshape(k // 512, 4)
    idx = np.arange(k)
    return np.exp2(a[idx // 512, idx % 128 // 32])


BF16 = ml_dtypes.bfloat16


def bf(x):
    return np.asarray(x, np.float32).astype(BF16)


def f64(x):
    return np.asarray(x).astype(np.float64)


E2M1 = np.array([0.0, 0.5, 1.0, 1.5, 2.0, 3.0, 4.0, 6.0, -0.0, -0.5, -1.0, -1.5, -2.0, -3.0, -4.0, -6.0])


def pack_weight(w, fmt):
    k, n = w.shape
    w = f64(bf(w)).reshape(k // 32, 32, n)
    amax = np.abs(w).max(1)
    if fmt == "e4m3":
        byte = np.frexp(amax)[1] - 1 + 127 - 7
    else:
        mant, ex = np.frexp(amax / 6.0)
        byte = np.where(mant > 0.5, ex, ex - 1) + 127
    byte = np.clip(np.where(amax > 0, byte, 1), 1, 254)
    scaled = (w * np.exp2(127.0 - byte)[:, None, :]).reshape(k, n).astype(np.float32)
    by_word = np.ascontiguousarray(scaled.reshape(k // 512, 128, 4, n).transpose(0, 1, 3, 2))
    if fmt == "e4m3":
        words = by_word.astype(ml_dtypes.float8_e4m3fn).view(np.uint8)
    else:
        c = by_word.astype(ml_dtypes.float4_e2m1fn).view(np.uint8) & 0xF
        words = c[..., 0::2] | (c[..., 1::2] << 4)
    return np.ascontiguousarray(words), np.ascontiguousarray(byte.astype(np.uint8).reshape(k // 512, 16, n))


def unpack_weight(words, scales, fmt):
    g, p, n, _ = words.shape
    if fmt == "e4m3":
        vals = np.ascontiguousarray(words).view(ml_dtypes.float8_e4m3fn).astype(np.float64)
    else:
        nib = np.empty((g, p, n, 4), np.uint8)
        nib[..., 0::2] = words & 0xF
        nib[..., 1::2] = words >> 4
        vals = E2M1[nib]
    vals = vals * np.repeat(np.exp2(scales.astype(np.float64) - 127.0), 8, axis=1)[..., None]
    return vals.transpose(0, 1, 3, 2).reshape(g * 512, n)

def pack4(w):
    words, scales = pack_weight(w, "e2m1")
    return words.reshape(words.shape[0], 128, -1), scales


def unpack4(words, scales):
    return unpack_weight(words.reshape(words.shape[0], 128, -1, 2), scales, "e2m1")


B, K, D, H1, H2, C = 256, 4, 2048, 1024, 512, 64
N = B * K


def setup_inputs():
    s = mx_kscale(D)
    nf1 = bf(np.random.standard_normal((N, D)) * s)
    nf2 = bf(np.random.standard_normal((N * K, D)) * s)
    w1_0_words, w1_0_scales = pack4(np.random.standard_normal((D, H1)) / np.sqrt(D) / s[:, None])
    w2_0_words, w2_0_scales = pack4(np.random.standard_normal((D, H1)) / np.sqrt(D) / s[:, None])
    return {"nf1": nf1,
            "nf2": nf2,
            "w1_0_words": w1_0_words,
            "w1_0_scales": w1_0_scales,
            "w2_0_words": w2_0_words,
            "w2_0_scales": w2_0_scales}


def sage_gcn(cur, neigh, w1, w2):
    b, d = cur.shape
    agg = neigh.reshape(b, -1, d).mean(axis=1)
    return np.maximum((mxq(cur, 1, "e4m3") @ w2) + (mxq(agg, 1, "e4m3") @ w1), 0.0)


def reference(nf1, nf2, w1_0_words, w1_0_scales, w2_0_words, w2_0_scales):
    return sage_gcn(f64(nf1), f64(nf2), unpack4(w1_0_words, w1_0_scales), unpack4(w2_0_words, w2_0_scales))

@@ -1,0 +1,181 @@
+from contextlib import ExitStack
+
+import concourse.mybir as mybir
+from concourse.masks import make_identity
+
+BF16 = mybir.dt.bfloat16
+F32 = mybir.dt.float32
+I32 = mybir.dt.int32
+U8 = mybir.dt.uint8
+U32 = mybir.dt.uint32
+FP8X4 = mybir.dt.float8_e4m3fn_x4
+FP4X4 = mybir.dt.float4_e2m1fn_x4
+
+P = 128
+PACK = 4
+K_PASS = P * PACK
+NODES = 1024
+NEIGHBOURS = 4
+D = 2048
+H = 1024
+GROUPS = D // K_PASS
+NODE_TILES = NODES // P
+NODES_PER_LOAD = P // NEIGHBOURS
+N_PASS = 512
+HALVES = H // N_PASS
+SCALE_ROWS = K_PASS // 32
+LOAD_AHEAD = NODE_TILES
+
+FLOPS = 2 * 2 * NODES * D * H + NODES * NEIGHBOURS * D
+
+
+def tile_graphsage_pa_kernel(
+    tc, nf1, nf2, w1_0_words, w1_0_scales, w2_0_words, w2_0_scales, out
+):
+    nc = tc.nc
+    with ExitStack() as ctx:
+        ctx.enter_context(tc.manual_schedule())
+        const = ctx.enter_context(tc.tile_pool(name="const", bufs=1))
+        feats = ctx.enter_context(tc.tile_pool(name="feats", bufs=1))
+        work = ctx.enter_context(tc.tile_pool(name="work", bufs=2))
+        stage = ctx.enter_context(tc.tile_pool(name="stage", bufs=4))
+        psum = ctx.enter_context(tc.psum_pool(name="psum", bufs=1))
+
+        def load_node_tile(m):
+            own = feats.tile([P, D], BF16, name="own%d" % m)
+            nc.sync.dma_start(out=own[:], in_=nf1[m * P : (m + 1) * P, :])
+            neigh = []
+            for a in range(NEIGHBOURS):
+                rows = feats.tile([P, D], BF16, name="neigh%d_%d" % (m, a))
+                first = (m * NEIGHBOURS + a) * P
+                nc.sync.dma_start(out=rows[:], in_=nf2[first : first + P, :])
+                neigh.append(rows)
+            return own, neigh
+
+        def load_scale_rows(label, scales_dram):
+            plane = const.tile([P, GROUPS, H], U8, name="plane_" + label, align_bytes=64)
+            nc.vector.memset(plane[:].bitcast(I32), 0)
+            for r in range(4):
+                nc.sync.dma_start(
+                    out=plane[r:P:32, :, :].bitcast(I32),
+                    in_=scales_dram.bitcast(I32)[:, r:SCALE_ROWS:4, :].rearrange("g q n -> q g n"),
+                )
+            return plane
+
+        def load_words(label, words_dram):
+            words = const.tile([P, GROUPS, 2 * H], U8, name="words_" + label, align_bytes=64)
+            nc.sync.dma_start(
+                out=words[:].bitcast(I32),
+                in_=words_dram.bitcast(I32).rearrange("g p b -> p g b"),
+            )
+            return words
+
+        loaded = [load_node_tile(0)]
+        own_plane = load_scale_rows("own", w2_0_scales)
+        agg_plane = load_scale_rows("agg", w1_0_scales)
+        own_words = load_words("own", w2_0_words)
+        agg_words = load_words("agg", w1_0_words)
+        for m in range(1, LOAD_AHEAD):
+            loaded.append(load_node_tile(m))
+
+        ident = const.tile([P, P], F32, name="ident")
+        make_identity(nc, ident[:])
+        group_of_row = const.tile([P, NODES_PER_LOAD], F32, name="group_of_row")
+        nc.vector.tensor_reduce(
+            out=group_of_row[:],
+            in_=ident[:].rearrange("p (n j) -> p n j", j=NEIGHBOURS),
+            axis=mybir.AxisListType.X,
+            op=mybir.AluOpType.add,
+        )
+        mean_weights = const.tile([P, NODES_PER_LOAD], BF16, name="mean_weights")
+        nc.vector.tensor_scalar_mul(mean_weights[:], group_of_row[:], 1.0 / NEIGHBOURS)
+
+        def quantise(label, grouped):
+            codes = work.tile([P, GROUPS, P], U32, tag="codes_" + label, align_bytes=64)
+            scales = work.tile([P, GROUPS, P], U8, tag="scales_" + label, align_bytes=64)
+            nc.vector.quantize_mx(
+                out=codes[:].rearrange("p g n -> p (g n)").bitcast(FP8X4),
+                scales=scales[:].rearrange("p g n -> p (g n)"),
+                in_=grouped[:].rearrange("p g n t -> p (g n t)"),
+            )
+            return codes, scales
+
+        def turn_own(own):
+            words = own[:].bitcast(F32)
+            grouped = work.tile([P, GROUPS, P, PACK], BF16, tag="grouped_own", align_bytes=64)
+            for pair in range(GROUPS // 2):
+                turned = psum.tile([P, 2, 2, P], F32, tag="turned_own%d" % pair)
+                for i in range(2):
+                    first = (2 * pair + i) * (K_PASS // 2)
+                    for u in range(2):
+                        nc.tensor.transpose(
+                            out=turned[:, i, u, :],
+                            in_=words[:, first + u : first + K_PASS // 2 : 2],
+                            identity=ident[:],
+                        )
+                nc.vector.tensor_copy(
+                    out=grouped[:, 2 * pair : 2 * pair + 2, :, :].bitcast(F32),
+                    in_=turned[:].rearrange("p i u n -> p i n u"),
+                )
+            return quantise("own", grouped)
+
+        def turn_mean(neigh):
+            grouped = work.tile([P, GROUPS, P, PACK], BF16, tag="grouped_agg", align_bytes=64)
+            turned = [
+                psum.tile([P, PACK, P], F32, name="turned_agg%d" % g) for g in range(GROUPS)
+            ]
+            for a in range(NEIGHBOURS):
+                nodes = slice(a * NODES_PER_LOAD, (a + 1) * NODES_PER_LOAD)
+                for g in range(GROUPS):
+                    for t in range(PACK):
+                        nc.tensor.matmul(
+                            out=turned[g][:, t, nodes],
+                            lhsT=neigh[a][:, g * K_PASS + t : (g + 1) * K_PASS : PACK],
+                            rhs=mean_weights[:],
+                            start=True,
+                            stop=True,
+                        )
+            for g in range(GROUPS):
+                by_node = turned[g][:].rearrange("p t n -> p n t")
+                if g % 2 == 0:
+                    nc.scalar.copy(out=grouped[:, g, :, :], in_=by_node)
+                else:
+                    nc.vector.tensor_copy(out=grouped[:, g, :, :], in_=by_node)
+            return quantise("agg", grouped)
+
+        def multiply(acc, x, w_words, w_plane, first, last):
+            codes, scales = x
+            for h in range(HALVES):
+                for g in range(GROUPS):
+                    nc.tensor.matmul_mx(
+                        out=acc[h][:],
+                        lhsT=codes[:, g, :].bitcast(FP8X4),
+                        lhsT_scale=scales[:, g, :],
+                        rhs=w_words[:, g, 2 * N_PASS * h : 2 * N_PASS * (h + 1)].bitcast(FP4X4),
+                        rhs_scale=w_plane[:, g, N_PASS * h : N_PASS * (h + 1)],
+                        start=first and g == 0,
+                        stop=last and g == GROUPS - 1,
+                    )
+
+        own_x = turn_own(loaded[0][0])
+        agg_x = turn_mean(loaded[0][1])
+        for m in range(NODE_TILES):
+            if m + LOAD_AHEAD < NODE_TILES:
+                loaded.append(load_node_tile(m + LOAD_AHEAD))
+            acc = [psum.tile([P, N_PASS], F32, name="acc%d" % h) for h in range(HALVES)]
+            if m + 1 < NODE_TILES:
+                next_own_x = turn_own(loaded[m + 1][0])
+            multiply(acc, own_x, own_words, own_plane, True, False)
+            if m + 1 < NODE_TILES:
+                next_agg_x = turn_mean(loaded[m + 1][1])
+            multiply(acc, agg_x, agg_words, agg_plane, False, True)
+            for h in range(HALVES):
+                result = stage.tile([P, N_PASS], F32, tag="result")
+                nc.scalar.activation(
+                    out=result[:], in_=acc[h][:], func=mybir.ActivationFunctionType.Relu
+                )
+                nc.scalar.dma_start(
+                    out=out[m * P : (m + 1) * P, h * N_PASS : (h + 1) * N_PASS], in_=result[:]
+                )
+            if m + 1 < NODE_TILES:
+                own_x, agg_x = next_own_x, next_agg_x

@@ -24,7 +24,7 @@ NODES_PER_LOAD = P // NEIGHBOURS
 N_PASS = 512
 HALVES = H // N_PASS
 SCALE_ROWS = K_PASS // 32
-LOAD_AHEAD = NODE_TILES
+RAW_BATCHES = 5
 
 FLOPS = 2 * 2 * NODES * D * H + NODES * NEIGHBOURS * D
 
@@ -36,21 +36,37 @@ def tile_graphsage_pa_kernel(
     with ExitStack() as ctx:
         ctx.enter_context(tc.manual_schedule())
         const = ctx.enter_context(tc.tile_pool(name="const", bufs=1))
-        feats = ctx.enter_context(tc.tile_pool(name="feats", bufs=1))
+        raw_own_pool = ctx.enter_context(tc.tile_pool(name="raw_own", bufs=RAW_BATCHES + 1))
+        raw_neigh_pool = ctx.enter_context(
+            tc.tile_pool(name="raw_neigh", bufs=RAW_BATCHES * NEIGHBOURS)
+        )
+        sorted_own_pool = ctx.enter_context(tc.tile_pool(name="sorted_own", bufs=3))
+        sorted_neigh_pool = ctx.enter_context(
+            tc.tile_pool(name="sorted_neigh", bufs=2 * NEIGHBOURS)
+        )
         work = ctx.enter_context(tc.tile_pool(name="work", bufs=2))
-        stage = ctx.enter_context(tc.tile_pool(name="stage", bufs=4))
+        stage = ctx.enter_context(tc.tile_pool(name="stage", bufs=8))
         psum = ctx.enter_context(tc.psum_pool(name="psum", bufs=1))
 
-        def load_node_tile(m):
-            own = feats.tile([P, D], BF16, name="own%d" % m)
-            nc.sync.dma_start(out=own[:], in_=nf1[m * P : (m + 1) * P, :])
-            neigh = []
+        raw_own = {}
+        raw_neigh = {}
+        sorted_own = {}
+        sorted_neigh = {}
+
+        def load_own(m):
+            rows = raw_own_pool.tile([P, D], BF16, tag="raw_own")
+            nc.sync.dma_start(out=rows[:], in_=nf1[m * P : (m + 1) * P, :])
+            raw_own[m] = rows
+
+        def load_batch(m):
+            if m + 1 < NODE_TILES:
+                load_own(m + 1)
+            raw_neigh[m] = []
             for a in range(NEIGHBOURS):
-                rows = feats.tile([P, D], BF16, name="neigh%d_%d" % (m, a))
+                rows = raw_neigh_pool.tile([P, D], BF16, tag="raw_neigh")
                 first = (m * NEIGHBOURS + a) * P
                 nc.sync.dma_start(out=rows[:], in_=nf2[first : first + P, :])
-                neigh.append(rows)
-            return own, neigh
+                raw_neigh[m].append(rows)
 
         def load_scale_rows(label, scales_dram):
             plane = const.tile([P, GROUPS, H], U8, name="plane_" + label, align_bytes=64)
@@ -70,13 +86,14 @@ def tile_graphsage_pa_kernel(
             )
             return words
 
-        loaded = [load_node_tile(0)]
+        load_own(0)
+        load_batch(0)
         own_plane = load_scale_rows("own", w2_0_scales)
         agg_plane = load_scale_rows("agg", w1_0_scales)
         own_words = load_words("own", w2_0_words)
         agg_words = load_words("agg", w1_0_words)
-        for m in range(1, LOAD_AHEAD):
-            loaded.append(load_node_tile(m))
+        for m in range(1, RAW_BATCHES):
+            load_batch(m)
 
         ident = const.tile([P, P], F32, name="ident")
         make_identity(nc, ident[:])
@@ -90,6 +107,25 @@ def tile_graphsage_pa_kernel(
         mean_weights = const.tile([P, NODES_PER_LOAD], BF16, name="mean_weights")
         nc.vector.tensor_scalar_mul(mean_weights[:], group_of_row[:], 1.0 / NEIGHBOURS)
 
+        def sort_words(copy, pool, tag, raw):
+            ordered = pool.tile([P, D], BF16, tag=tag)
+            copy(
+                out=ordered[:].bitcast(F32).rearrange("p (g u c) -> p g u c", g=GROUPS, u=2),
+                in_=raw[:].bitcast(F32).rearrange("p (g c u) -> p g u c", g=GROUPS, u=2),
+            )
+            return ordered
+
+        def sort_own(m):
+            sorted_own[m] = sort_words(nc.scalar.copy, sorted_own_pool, "sorted_own", raw_own[m])
+
+        def sort_batch(m):
+            if m + 1 < NODE_TILES:
+                sort_own(m + 1)
+            sorted_neigh[m] = [
+                sort_words(nc.vector.tensor_copy, sorted_neigh_pool, "sorted_neigh", rows)
+                for rows in raw_neigh[m]
+            ]
+
         def quantise(label, grouped):
             codes = work.tile([P, GROUPS, P], U32, tag="codes_" + label, align_bytes=64)
             scales = work.tile([P, GROUPS, P], U8, tag="scales_" + label, align_bytes=64)
@@ -100,41 +136,47 @@ def tile_graphsage_pa_kernel(
             )
             return codes, scales
 
-        def turn_own(own):
-            words = own[:].bitcast(F32)
+        def turn_own(m):
+            words = sorted_own[m][:].bitcast(F32)
             grouped = work.tile([P, GROUPS, P, PACK], BF16, tag="grouped_own", align_bytes=64)
             for pair in range(GROUPS // 2):
                 turned = psum.tile([P, 2, 2, P], F32, tag="turned_own%d" % pair)
                 for i in range(2):
-                    first = (2 * pair + i) * (K_PASS // 2)
                     for u in range(2):
+                        first = ((2 * pair + i) * 2 + u) * P
                         nc.tensor.transpose(
                             out=turned[:, i, u, :],
-                            in_=words[:, first + u : first + K_PASS // 2 : 2],
+                            in_=words[:, first : first + P],
                             identity=ident[:],
                         )
-                nc.vector.tensor_copy(
+                nc.scalar.copy(
                     out=grouped[:, 2 * pair : 2 * pair + 2, :, :].bitcast(F32),
                     in_=turned[:].rearrange("p i u n -> p i n u"),
                 )
             return quantise("own", grouped)
 
-        def turn_mean(neigh):
-            grouped = work.tile([P, GROUPS, P, PACK], BF16, tag="grouped_agg", align_bytes=64)
+        def turn_mean(m):
             turned = [
                 psum.tile([P, PACK, P], F32, name="turned_agg%d" % g) for g in range(GROUPS)
             ]
             for a in range(NEIGHBOURS):
                 nodes = slice(a * NODES_PER_LOAD, (a + 1) * NODES_PER_LOAD)
+                by_t = sorted_neigh[m][a][:].rearrange(
+                    "p (g u c e) -> p g u c e", g=GROUPS, u=2, e=2
+                )
                 for g in range(GROUPS):
                     for t in range(PACK):
                         nc.tensor.matmul(
                             out=turned[g][:, t, nodes],
-                            lhsT=neigh[a][:, g * K_PASS + t : (g + 1) * K_PASS : PACK],
+                            lhsT=by_t[:, g, t // 2, :, t % 2],
                             rhs=mean_weights[:],
                             start=True,
                             stop=True,
                         )
+            return turned
+
+        def quantise_mean(turned):
+            grouped = work.tile([P, GROUPS, P, PACK], BF16, tag="grouped_agg", align_bytes=64)
             for g in range(GROUPS):
                 by_node = turned[g][:].rearrange("p t n -> p n t")
                 if g % 2 == 0:
@@ -157,25 +199,27 @@ def tile_graphsage_pa_kernel(
                         stop=last and g == GROUPS - 1,
                     )
 
-        own_x = turn_own(loaded[0][0])
-        agg_x = turn_mean(loaded[0][1])
+        sort_own(0)
+        sort_batch(0)
+        own_x = turn_own(0)
+        turned_mean = turn_mean(0)
         for m in range(NODE_TILES):
-            if m + LOAD_AHEAD < NODE_TILES:
-                loaded.append(load_node_tile(m + LOAD_AHEAD))
+            agg_x = quantise_mean(turned_mean)
             acc = [psum.tile([P, N_PASS], F32, name="acc%d" % h) for h in range(HALVES)]
-            if m + 1 < NODE_TILES:
-                next_own_x = turn_own(loaded[m + 1][0])
             multiply(acc, own_x, own_words, own_plane, True, False)
             if m + 1 < NODE_TILES:
-                next_agg_x = turn_mean(loaded[m + 1][1])
+                sort_batch(m + 1)
+                if m + RAW_BATCHES < NODE_TILES:
+                    load_batch(m + RAW_BATCHES)
+                own_x = turn_own(m + 1)
             multiply(acc, agg_x, agg_words, agg_plane, False, True)
             for h in range(HALVES):
                 result = stage.tile([P, N_PASS], F32, tag="result")
                 nc.scalar.activation(
                     out=result[:], in_=acc[h][:], func=mybir.ActivationFunctionType.Relu
                 )
-                nc.scalar.dma_start(
+                nc.sync.dma_start(
                     out=out[m * P : (m + 1) * P, h * N_PASS : (h + 1) * N_PASS], in_=result[:]
                 )
             if m + 1 < NODE_TILES:
-                own_x, agg_x = next_own_x, next_agg_x
+                turned_mean = turn_mean(m + 1)

@@ -59,14 +59,14 @@ def tile_graphsage_pa_kernel(
             raw_own[m] = rows
 
         def load_batch(m):
-            if m + 1 < NODE_TILES:
-                load_own(m + 1)
             raw_neigh[m] = []
             for a in range(NEIGHBOURS):
                 rows = raw_neigh_pool.tile([P, D], BF16, tag="raw_neigh")
                 first = (m * NEIGHBOURS + a) * P
                 nc.sync.dma_start(out=rows[:], in_=nf2[first : first + P, :])
                 raw_neigh[m].append(rows)
+            if m + 1 < NODE_TILES:
+                load_own(m + 1)
 
         def load_scale_rows(label, scales_dram):
             plane = const.tile([P, GROUPS, H], U8, name="plane_" + label, align_bytes=64)
@@ -119,8 +119,6 @@ def tile_graphsage_pa_kernel(
             sorted_own[m] = sort_words(nc.scalar.copy, sorted_own_pool, "sorted_own", raw_own[m])
 
         def sort_batch(m):
-            if m + 1 < NODE_TILES:
-                sort_own(m + 1)
             sorted_neigh[m] = [
                 sort_words(nc.vector.tensor_copy, sorted_neigh_pool, "sorted_neigh", rows)
                 for rows in raw_neigh[m]
@@ -203,6 +201,7 @@ def tile_graphsage_pa_kernel(
         sort_batch(0)
         own_x = turn_own(0)
         turned_mean = turn_mean(0)
+        sort_own(1)
         for m in range(NODE_TILES):
             agg_x = quantise_mean(turned_mean)
             acc = [psum.tile([P, N_PASS], F32, name="acc%d" % h) for h in range(HALVES)]
@@ -221,5 +220,7 @@ def tile_graphsage_pa_kernel(
                 nc.sync.dma_start(
                     out=out[m * P : (m + 1) * P, h * N_PASS : (h + 1) * N_PASS], in_=result[:]
                 )
+            if m + 2 < NODE_TILES:
+                sort_own(m + 2)
             if m + 1 < NODE_TILES:
                 turned_mean = turn_mean(m + 1)

@@ -59,13 +59,15 @@ def tile_graphsage_pa_kernel(
             raw_own[m] = rows
 
         def load_batch(m):
+            if m + 1 < NODE_TILES and m != 1:
+                load_own(m + 1)
             raw_neigh[m] = []
             for a in range(NEIGHBOURS):
                 rows = raw_neigh_pool.tile([P, D], BF16, tag="raw_neigh")
                 first = (m * NEIGHBOURS + a) * P
                 nc.sync.dma_start(out=rows[:], in_=nf2[first : first + P, :])
                 raw_neigh[m].append(rows)
-            if m + 1 < NODE_TILES:
+            if m == 1:
                 load_own(m + 1)
 
         def load_scale_rows(label, scales_dram):
@@ -119,6 +121,8 @@ def tile_graphsage_pa_kernel(
             sorted_own[m] = sort_words(nc.scalar.copy, sorted_own_pool, "sorted_own", raw_own[m])
 
         def sort_batch(m):
+            if m + 1 < NODE_TILES and m != 1:
+                sort_own(m + 1)
             sorted_neigh[m] = [
                 sort_words(nc.vector.tensor_copy, sorted_neigh_pool, "sorted_neigh", rows)
                 for rows in raw_neigh[m]
@@ -201,7 +205,6 @@ def tile_graphsage_pa_kernel(
         sort_batch(0)
         own_x = turn_own(0)
         turned_mean = turn_mean(0)
-        sort_own(1)
         for m in range(NODE_TILES):
             agg_x = quantise_mean(turned_mean)
             acc = [psum.tile([P, N_PASS], F32, name="acc%d" % h) for h in range(HALVES)]
@@ -220,7 +223,7 @@ def tile_graphsage_pa_kernel(
                 nc.sync.dma_start(
                     out=out[m * P : (m + 1) * P, h * N_PASS : (h + 1) * N_PASS], in_=result[:]
                 )
-            if m + 2 < NODE_TILES:
-                sort_own(m + 2)
+            if m == 0:
+                sort_own(2)
             if m + 1 < NODE_TILES:
                 turned_mean = turn_mean(m + 1)

@@ -71,7 +71,7 @@ def tile_graphsage_pa_kernel(
                 load_own(m + 1)
 
         def load_scale_rows(label, scales_dram):
-            plane = const.tile([P, GROUPS, H], U8, name="plane_" + label, align_bytes=64)
+            plane = const.tile([P, GROUPS, H], U8, name="plane_" + label, align_bytes=256)
             nc.vector.memset(plane[:].bitcast(I32), 0)
             for r in range(4):
                 nc.sync.dma_start(
@@ -81,7 +81,7 @@ def tile_graphsage_pa_kernel(
             return plane
 
         def load_words(label, words_dram):
-            words = const.tile([P, GROUPS, 2 * H], U8, name="words_" + label, align_bytes=64)
+            words = const.tile([P, GROUPS, 2 * H], U8, name="words_" + label, align_bytes=256)
             nc.sync.dma_start(
                 out=words[:].bitcast(I32),
                 in_=words_dram.bitcast(I32).rearrange("g p b -> p g b"),
@@ -129,8 +129,8 @@ def tile_graphsage_pa_kernel(
             ]
 
         def quantise(label, grouped):
-            codes = work.tile([P, GROUPS, P], U32, tag="codes_" + label, align_bytes=64)
-            scales = work.tile([P, GROUPS, P], U8, tag="scales_" + label, align_bytes=64)
+            codes = work.tile([P, GROUPS, P], U32, tag="codes_" + label, align_bytes=256)
+            scales = work.tile([P, GROUPS, P], U8, tag="scales_" + label, align_bytes=256)
             nc.vector.quantize_mx(
                 out=codes[:].rearrange("p g n -> p (g n)").bitcast(FP8X4),
                 scales=scales[:].rearrange("p g n -> p (g n)"),
@@ -140,7 +140,7 @@ def tile_graphsage_pa_kernel(
 
         def turn_own(m):
             words = sorted_own[m][:].bitcast(F32)
-            grouped = work.tile([P, GROUPS, P, PACK], BF16, tag="grouped_own", align_bytes=64)
+            grouped = work.tile([P, GROUPS, P, PACK], BF16, tag="grouped_own", align_bytes=256)
             for pair in range(GROUPS // 2):
                 turned = psum.tile([P, 2, 2, P], F32, tag="turned_own%d" % pair)
                 for i in range(2):
@@ -178,7 +178,7 @@ def tile_graphsage_pa_kernel(
             return turned
 
         def quantise_mean(turned):
-            grouped = work.tile([P, GROUPS, P, PACK], BF16, tag="grouped_agg", align_bytes=64)
+            grouped = work.tile([P, GROUPS, P, PACK], BF16, tag="grouped_agg", align_bytes=256)
             for g in range(GROUPS):
                 by_node = turned[g][:].rearrange("p t n -> p n t")
                 if g % 2 == 0:

@@ -24,7 +24,7 @@ NODES_PER_LOAD = P // NEIGHBOURS
 N_PASS = 512
 HALVES = H // N_PASS
 SCALE_ROWS = K_PASS // 32
-RAW_BATCHES = 5
+PARKED = 7
 
 FLOPS = 2 * 2 * NODES * D * H + NODES * NEIGHBOURS * D
 
@@ -36,49 +36,50 @@ def tile_graphsage_pa_kernel(
     with ExitStack() as ctx:
         ctx.enter_context(tc.manual_schedule())
         const = ctx.enter_context(tc.tile_pool(name="const", bufs=1))
-        raw_own_pool = ctx.enter_context(tc.tile_pool(name="raw_own", bufs=RAW_BATCHES + 1))
-        raw_neigh_pool = ctx.enter_context(
-            tc.tile_pool(name="raw_neigh", bufs=RAW_BATCHES * NEIGHBOURS)
-        )
-        sorted_own_pool = ctx.enter_context(tc.tile_pool(name="sorted_own", bufs=3))
+        raw_own_pool = ctx.enter_context(tc.tile_pool(name="raw_own", bufs=6))
+        raw_neigh_pool = ctx.enter_context(tc.tile_pool(name="raw_neigh", bufs=4 * NEIGHBOURS))
+        sorted_own_pool = ctx.enter_context(tc.tile_pool(name="sorted_own", bufs=4))
         sorted_neigh_pool = ctx.enter_context(
             tc.tile_pool(name="sorted_neigh", bufs=2 * NEIGHBOURS)
         )
         work = ctx.enter_context(tc.tile_pool(name="work", bufs=2))
-        stage = ctx.enter_context(tc.tile_pool(name="stage", bufs=8))
+        own_ops = ctx.enter_context(tc.tile_pool(name="own_ops", bufs=4))
+        result_pool = ctx.enter_context(tc.tile_pool(name="result", bufs=NODE_TILES))
         psum = ctx.enter_context(tc.psum_pool(name="psum", bufs=1))
 
         raw_own = {}
         raw_neigh = {}
         sorted_own = {}
         sorted_neigh = {}
+        own_x = {}
+        agg_x = {}
+        results = {}
+        mean_acc = {}
 
         def load_own(m):
             rows = raw_own_pool.tile([P, D], BF16, tag="raw_own")
             nc.sync.dma_start(out=rows[:], in_=nf1[m * P : (m + 1) * P, :])
             raw_own[m] = rows
 
-        def load_batch(m):
-            if m + 1 < NODE_TILES and m != 1:
-                load_own(m + 1)
+        def load_neigh(m):
             raw_neigh[m] = []
             for a in range(NEIGHBOURS):
                 rows = raw_neigh_pool.tile([P, D], BF16, tag="raw_neigh")
                 first = (m * NEIGHBOURS + a) * P
                 nc.sync.dma_start(out=rows[:], in_=nf2[first : first + P, :])
                 raw_neigh[m].append(rows)
-            if m == 1:
-                load_own(m + 1)
 
-        def load_scale_rows(label, scales_dram):
+        def zero_plane(label):
             plane = const.tile([P, GROUPS, H], U8, name="plane_" + label, align_bytes=256)
             nc.vector.memset(plane[:].bitcast(I32), 0)
+            return plane
+
+        def load_scale_rows(plane, scales_dram):
             for r in range(4):
                 nc.sync.dma_start(
                     out=plane[r:P:32, :, :].bitcast(I32),
                     in_=scales_dram.bitcast(I32)[:, r:SCALE_ROWS:4, :].rearrange("g q n -> q g n"),
                 )
-            return plane
 
         def load_words(label, words_dram):
             words = const.tile([P, GROUPS, 2 * H], U8, name="words_" + label, align_bytes=256)
@@ -89,13 +90,13 @@ def tile_graphsage_pa_kernel(
             return words
 
         load_own(0)
-        load_batch(0)
-        own_plane = load_scale_rows("own", w2_0_scales)
-        agg_plane = load_scale_rows("agg", w1_0_scales)
+        load_own(1)
+        own_plane = zero_plane("own")
+        load_scale_rows(own_plane, w2_0_scales)
         own_words = load_words("own", w2_0_words)
-        agg_words = load_words("agg", w1_0_words)
-        for m in range(1, RAW_BATCHES):
-            load_batch(m)
+        for m in range(2, PARKED):
+            load_own(m)
+        agg_plane = zero_plane("agg")
 
         ident = const.tile([P, P], F32, name="ident")
         make_identity(nc, ident[:])
@@ -117,20 +118,21 @@ def tile_graphsage_pa_kernel(
             )
             return ordered
 
-        def sort_own(m):
-            sorted_own[m] = sort_words(nc.scalar.copy, sorted_own_pool, "sorted_own", raw_own[m])
+        def sort_neigh(m, blocks=range(NEIGHBOURS)):
+            for a in blocks:
+                rows = raw_neigh[m][a]
+                sorted_neigh.setdefault(m, []).append(
+                    sort_words(
+                        nc.vector.tensor_copy,
+                        sorted_neigh_pool,
+                        "sorted_neigh",
+                        rows,
+                    )
+                )
 
-        def sort_batch(m):
-            if m + 1 < NODE_TILES and m != 1:
-                sort_own(m + 1)
-            sorted_neigh[m] = [
-                sort_words(nc.vector.tensor_copy, sorted_neigh_pool, "sorted_neigh", rows)
-                for rows in raw_neigh[m]
-            ]
-
-        def quantise(label, grouped):
-            codes = work.tile([P, GROUPS, P], U32, tag="codes_" + label, align_bytes=256)
-            scales = work.tile([P, GROUPS, P], U8, tag="scales_" + label, align_bytes=256)
+        def quantise(pool, label, grouped):
+            codes = pool.tile([P, GROUPS, P], U32, tag="codes_" + label, align_bytes=256)
+            scales = pool.tile([P, GROUPS, P], U8, tag="scales_" + label, align_bytes=256)
             nc.vector.quantize_mx(
                 out=codes[:].rearrange("p g n -> p (g n)").bitcast(FP8X4),
                 scales=scales[:].rearrange("p g n -> p (g n)"),
@@ -138,11 +140,16 @@ def tile_graphsage_pa_kernel(
             )
             return codes, scales
 
+        def sort_own(m):
+            sorted_own[m] = sort_words(
+                nc.vector.tensor_copy, sorted_own_pool, "sorted_own", raw_own[m]
+            )
+
         def turn_own(m):
             words = sorted_own[m][:].bitcast(F32)
             grouped = work.tile([P, GROUPS, P, PACK], BF16, tag="grouped_own", align_bytes=256)
             for pair in range(GROUPS // 2):
-                turned = psum.tile([P, 2, 2, P], F32, tag="turned_own%d" % pair)
+                turned = psum.tile([P, 2, 2, P], F32, tag="turn%d" % (2 * (m % 2) + pair))
                 for i in range(2):
                     for u in range(2):
                         first = ((2 * pair + i) * 2 + u) * P
@@ -151,79 +158,157 @@ def tile_graphsage_pa_kernel(
                             in_=words[:, first : first + P],
                             identity=ident[:],
                         )
-                nc.scalar.copy(
+                copy = nc.scalar.copy if pair == 0 else nc.vector.tensor_copy
+                copy(
                     out=grouped[:, 2 * pair : 2 * pair + 2, :, :].bitcast(F32),
                     in_=turned[:].rearrange("p i u n -> p i n u"),
                 )
-            return quantise("own", grouped)
+            own_x[m] = quantise(own_ops, "own", grouped)
 
         def turn_mean(m):
-            turned = [
-                psum.tile([P, PACK, P], F32, name="turned_agg%d" % g) for g in range(GROUPS)
-            ]
-            for a in range(NEIGHBOURS):
+            grouped = work.tile([P, GROUPS, P, PACK], BF16, tag="grouped_agg", align_bytes=256)
+            turned = []
+            for g in range(GROUPS):
+                bank = psum.tile([P, PACK, P], F32, tag="turn%d" % g)
+                turned.append(bank)
+            order = [(a, g) for g in range(GROUPS) for a in range(NEIGHBOURS)] if m != 7 else [(a, g) for a in range(NEIGHBOURS) for g in range(GROUPS)]
+            for a, g in order:
                 nodes = slice(a * NODES_PER_LOAD, (a + 1) * NODES_PER_LOAD)
                 by_t = sorted_neigh[m][a][:].rearrange(
                     "p (g u c e) -> p g u c e", g=GROUPS, u=2, e=2
                 )
-                for g in range(GROUPS):
-                    for t in range(PACK):
-                        nc.tensor.matmul(
-                            out=turned[g][:, t, nodes],
-                            lhsT=by_t[:, g, t // 2, :, t % 2],
-                            rhs=mean_weights[:],
-                            start=True,
-                            stop=True,
-                        )
-            return turned
-
-        def quantise_mean(turned):
-            grouped = work.tile([P, GROUPS, P, PACK], BF16, tag="grouped_agg", align_bytes=256)
-            for g in range(GROUPS):
-                by_node = turned[g][:].rearrange("p t n -> p n t")
-                if g % 2 == 0:
-                    nc.scalar.copy(out=grouped[:, g, :, :], in_=by_node)
-                else:
-                    nc.vector.tensor_copy(out=grouped[:, g, :, :], in_=by_node)
-            return quantise("agg", grouped)
-
-        def multiply(acc, x, w_words, w_plane, first, last):
-            codes, scales = x
-            for h in range(HALVES):
-                for g in range(GROUPS):
-                    nc.tensor.matmul_mx(
-                        out=acc[h][:],
-                        lhsT=codes[:, g, :].bitcast(FP8X4),
-                        lhsT_scale=scales[:, g, :],
-                        rhs=w_words[:, g, 2 * N_PASS * h : 2 * N_PASS * (h + 1)].bitcast(FP4X4),
-                        rhs_scale=w_plane[:, g, N_PASS * h : N_PASS * (h + 1)],
-                        start=first and g == 0,
-                        stop=last and g == GROUPS - 1,
+                for t in range(PACK):
+                    nc.tensor.matmul(
+                        out=turned[g][:, t, nodes],
+                        lhsT=by_t[:, g, t // 2, :, t % 2],
+                        rhs=mean_weights[:],
+                        start=True,
+                        stop=True,
                     )
+            for g in range(GROUPS):
+                copy = nc.vector.tensor_copy if (m in (0, 7) and g % 2 == 1) else nc.scalar.copy
+                copy(out=grouped[:, g, :, :], in_=turned[g][:].rearrange("p t n -> p n t"))
+            return grouped
 
-        sort_own(0)
-        sort_batch(0)
-        own_x = turn_own(0)
-        turned_mean = turn_mean(0)
-        for m in range(NODE_TILES):
-            agg_x = quantise_mean(turned_mean)
-            acc = [psum.tile([P, N_PASS], F32, name="acc%d" % h) for h in range(HALVES)]
-            multiply(acc, own_x, own_words, own_plane, True, False)
-            if m + 1 < NODE_TILES:
-                sort_batch(m + 1)
-                if m + RAW_BATCHES < NODE_TILES:
-                    load_batch(m + RAW_BATCHES)
-                own_x = turn_own(m + 1)
-            multiply(acc, agg_x, agg_words, agg_plane, False, True)
+        def quantise_mean(m, grouped):
+            agg_x[m] = quantise(work, "agg", grouped)
+
+        def new_acc(s):
+            banks = []
             for h in range(HALVES):
-                result = stage.tile([P, N_PASS], F32, tag="result")
+                bank = psum.tile([P, N_PASS], F32, tag="acc%d" % (2 * s + h))
+                banks.append(bank)
+            return banks
+
+        def multiply(acc, h, x, w_words, w_plane, first, last):
+            codes, scales = x
+            for g in range(GROUPS):
+                nc.tensor.matmul_mx(
+                    out=acc[h][:],
+                    lhsT=codes[:, g, :].bitcast(FP8X4),
+                    lhsT_scale=scales[:, g, :],
+                    rhs=w_words[:, g, 2 * N_PASS * h : 2 * N_PASS * (h + 1)].bitcast(FP4X4),
+                    rhs_scale=w_plane[:, g, N_PASS * h : N_PASS * (h + 1)],
+                    start=first and g == 0,
+                    stop=last and g == GROUPS - 1,
+                )
+
+        def park_own_product(m):
+            acc = new_acc(m % 2)
+            result = result_pool.tile([P, H], F32, tag="result")
+            results[m] = result
+            for h in range(HALVES):
+                multiply(acc, h, own_x[m], own_words, own_plane, True, True)
+                nc.scalar.copy(out=results[m][:, h * N_PASS : (h + 1) * N_PASS], in_=acc[h][:])
+
+        def store(m):
+            for h in range(HALVES):
+                cols = slice(h * N_PASS, (h + 1) * N_PASS)
+                nc.sync.dma_start(out=out[m * P : (m + 1) * P, cols], in_=results[m][:, cols])
+
+        def multiply_mean(m):
+            mean_acc[m] = new_acc(0)
+            for h in range(HALVES):
+                multiply(mean_acc[m], h, agg_x[m], agg_words, agg_plane, True, True)
+
+        def add_parked(m):
+            for h in range(HALVES):
+                cols = slice(h * N_PASS, (h + 1) * N_PASS)
+                nc.vector.tensor_tensor(
+                    out=results[m][:, cols],
+                    in0=mean_acc[m][h][:],
+                    in1=results[m][:, cols],
+                    op=mybir.AluOpType.add,
+                )
+
+        def relu(m):
+            for h in range(HALVES):
+                cols = slice(h * N_PASS, (h + 1) * N_PASS)
                 nc.scalar.activation(
-                    out=result[:], in_=acc[h][:], func=mybir.ActivationFunctionType.Relu
+                    out=results[m][:, cols],
+                    in_=results[m][:, cols],
+                    func=mybir.ActivationFunctionType.Relu,
                 )
-                nc.sync.dma_start(
-                    out=out[m * P : (m + 1) * P, h * N_PASS : (h + 1) * N_PASS], in_=result[:]
-                )
-            if m == 0:
-                sort_own(2)
-            if m + 1 < NODE_TILES:
-                turned_mean = turn_mean(m + 1)
+
+        LAST = NODE_TILES - 1
+        sort_own(0)
+        load_own(6)
+        sort_own(1)
+        load_own(7)
+        load_scale_rows(agg_plane, w1_0_scales)
+        agg_words = load_words("agg", w1_0_words)
+        for m in range(4):
+            load_neigh(m)
+        turn_own(0)
+        turn_own(1)
+        sort_own(2)
+        sort_own(3)
+        for k in range(PARKED):
+            if k == 3:
+                sort_neigh(0, (0, 1))
+            if k == 5:
+                sort_neigh(0, (2, 3))
+                load_neigh(4)
+                sort_neigh(1, (0, 1))
+            park_own_product(k)
+            if k % 2 == 0 and k + 2 < NODE_TILES:
+                turn_own(k + 2)
+                turn_own(k + 3)
+                if k + 4 < NODE_TILES:
+                    sort_own(k + 4)
+                    sort_own(k + 5)
+        grouped = turn_mean(0)
+        quantise_mean(0, grouped)
+        sort_neigh(1, (2, 3))
+        load_neigh(5)
+        last_acc = new_acc(1)
+        for h in range(HALVES):
+            multiply(last_acc, h, own_x[LAST], own_words, own_plane, True, False)
+        for m in range(LAST):
+            if m > 0:
+                add_parked(m - 1)
+            grouped = turn_mean(m + 1)
+            if m + 2 < NODE_TILES:
+                sort_neigh(m + 2, (0, 1, 2))
+            quantise_mean(m + 1, grouped)
+            if m + 2 < NODE_TILES:
+                sort_neigh(m + 2, (3,))
+                if m + 6 < NODE_TILES:
+                    load_neigh(m + 6)
+            multiply_mean(m)
+            if m > 0:
+                relu(m - 1)
+            if m > 2:
+                store(m - 3)
+        add_parked(LAST - 1)
+        result = result_pool.tile([P, H], F32, tag="result")
+        results[LAST] = result
+        relu(LAST - 1)
+        for h in range(HALVES):
+            cols = slice(h * N_PASS, (h + 1) * N_PASS)
+            multiply(last_acc, h, agg_x[LAST], agg_words, agg_plane, False, True)
+            nc.scalar.activation(
+                out=results[LAST][:, cols], in_=last_acc[h][:], func=mybir.ActivationFunctionType.Relu
+            )
+        for m in range(LAST - 3, NODE_TILES):
+            store(m)

@@ -113,8 +113,8 @@ def tile_graphsage_pa_kernel(
         def sort_words(copy, pool, tag, raw):
             ordered = pool.tile([P, D], BF16, tag=tag)
             copy(
-                out=ordered[:].bitcast(F32).rearrange("p (g u c) -> p g u c", g=GROUPS, u=2),
-                in_=raw[:].bitcast(F32).rearrange("p (g c u) -> p g u c", g=GROUPS, u=2),
+                out=ordered[:].bitcast(F32).rearrange("p (g u c i) -> p g c u i", g=GROUPS, u=2, i=4),
+                in_=raw[:].bitcast(F32).rearrange("p (g c i u) -> p g c u i", g=GROUPS, u=2, i=4),
             )
             return ordered
 

@@ -120,15 +120,16 @@ def tile_graphsage_pa_kernel(
 
         def sort_neigh(m, blocks=range(NEIGHBOURS)):
             for a in blocks:
-                rows = raw_neigh[m][a]
-                sorted_neigh.setdefault(m, []).append(
-                    sort_words(
-                        nc.vector.tensor_copy,
-                        sorted_neigh_pool,
-                        "sorted_neigh",
-                        rows,
+                if a == 3 and m >= 1:
+                    by_t = raw_neigh[m][a][:].rearrange(
+                        "p (g c u e) -> p g u c e", g=GROUPS, u=2, e=2
                     )
-                )
+                else:
+                    ordered = sort_words(
+                        nc.vector.tensor_copy, sorted_neigh_pool, "sorted_neigh", raw_neigh[m][a]
+                    )
+                    by_t = ordered[:].rearrange("p (g u c e) -> p g u c e", g=GROUPS, u=2, e=2)
+                sorted_neigh.setdefault(m, []).append(by_t)
 
         def quantise(pool, label, grouped):
             codes = pool.tile([P, GROUPS, P], U32, tag="codes_" + label, align_bytes=256)
@@ -174,9 +175,7 @@ def tile_graphsage_pa_kernel(
             order = [(a, g) for g in range(GROUPS) for a in range(NEIGHBOURS)] if m != 7 else [(a, g) for a in range(NEIGHBOURS) for g in range(GROUPS)]
             for a, g in order:
                 nodes = slice(a * NODES_PER_LOAD, (a + 1) * NODES_PER_LOAD)
-                by_t = sorted_neigh[m][a][:].rearrange(
-                    "p (g u c e) -> p g u c e", g=GROUPS, u=2, e=2
-                )
+                by_t = sorted_neigh[m][a]
                 for t in range(PACK):
                     nc.tensor.matmul(
                         out=turned[g][:, t, nodes],
@@ -268,7 +267,6 @@ def tile_graphsage_pa_kernel(
                 sort_neigh(0, (0, 1))
             if k == 5:
                 sort_neigh(0, (2, 3))
-                load_neigh(4)
                 sort_neigh(1, (0, 1))
             park_own_product(k)
             if k % 2 == 0 and k + 2 < NODE_TILES:
@@ -280,7 +278,7 @@ def tile_graphsage_pa_kernel(
         grouped = turn_mean(0)
         quantise_mean(0, grouped)
         sort_neigh(1, (2, 3))
-        load_neigh(5)
+        load_neigh(4)
         last_acc = new_acc(1)
         for h in range(HALVES):
             multiply(last_acc, h, own_x[LAST], own_words, own_plane, True, False)
@@ -293,8 +291,8 @@ def tile_graphsage_pa_kernel(
             quantise_mean(m + 1, grouped)
             if m + 2 < NODE_TILES:
                 sort_neigh(m + 2, (3,))
-                if m + 6 < NODE_TILES:
-                    load_neigh(m + 6)
+            if m + 5 < NODE_TILES:
+                load_neigh(m + 5)
             multiply_mean(m)
             if m > 0:
                 relu(m - 1)

@@ -25,6 +25,7 @@ N_PASS = 512
 HALVES = H // N_PASS
 SCALE_ROWS = K_PASS // 32
 PARKED = 7
+OWN_PIECES = [slice(0, GROUPS // 2), slice(GROUPS // 2, GROUPS)]
 
 FLOPS = 2 * 2 * NODES * D * H + NODES * NEIGHBOURS * D
 
@@ -55,6 +56,7 @@ def tile_graphsage_pa_kernel(
         agg_x = {}
         results = {}
         mean_acc = {}
+        own_acc = {}
 
         def load_own(m):
             rows = raw_own_pool.tile([P, D], BF16, tag="raw_own")
@@ -81,20 +83,21 @@ def tile_graphsage_pa_kernel(
                     in_=scales_dram.bitcast(I32)[:, r:SCALE_ROWS:4, :].rearrange("g q n -> q g n"),
                 )
 
-        def load_words(label, words_dram):
+        def load_words(label, words_dram, pieces):
             words = const.tile([P, GROUPS, 2 * H], U8, name="words_" + label, align_bytes=256)
-            nc.sync.dma_start(
-                out=words[:].bitcast(I32),
-                in_=words_dram.bitcast(I32).rearrange("g p b -> p g b"),
-            )
+            for groups in pieces:
+                nc.sync.dma_start(
+                    out=words[:, groups, :].bitcast(I32),
+                    in_=words_dram.bitcast(I32)[groups, :, :].rearrange("g p b -> p g b"),
+                )
             return words
 
         load_own(0)
         load_own(1)
         own_plane = zero_plane("own")
         load_scale_rows(own_plane, w2_0_scales)
-        own_words = load_words("own", w2_0_words)
-        for m in range(2, PARKED):
+        own_words = load_words("own", w2_0_words, OWN_PIECES)
+        for m in range(2, 6):
             load_own(m)
         agg_plane = zero_plane("agg")
 
@@ -199,9 +202,9 @@ def tile_graphsage_pa_kernel(
                 banks.append(bank)
             return banks
 
-        def multiply(acc, h, x, w_words, w_plane, first, last):
+        def multiply(acc, h, x, w_words, w_plane, first, last, groups=range(GROUPS)):
             codes, scales = x
-            for g in range(GROUPS):
+            for g in groups:
                 nc.tensor.matmul_mx(
                     out=acc[h][:],
                     lhsT=codes[:, g, :].bitcast(FP8X4),
@@ -212,17 +215,30 @@ def tile_graphsage_pa_kernel(
                     stop=last and g == GROUPS - 1,
                 )
 
-        def park_own_product(m):
-            acc = new_acc(m % 2)
-            result = result_pool.tile([P, H], F32, tag="result")
-            results[m] = result
-            for h in range(HALVES):
-                multiply(acc, h, own_x[m], own_words, own_plane, True, True)
-                nc.scalar.copy(out=results[m][:, h * N_PASS : (h + 1) * N_PASS], in_=acc[h][:])
+        def open_own_product(m):
+            banks = new_acc(m % 2)
+            own_acc[m] = banks
 
-        def store(m):
+        def multiply_own(m, groups=range(GROUPS)):
             for h in range(HALVES):
-                cols = slice(h * N_PASS, (h + 1) * N_PASS)
+                multiply(own_acc[m], h, own_x[m], own_words, own_plane, True, True, groups)
+                if GROUPS - 1 in groups:
+                    park(m, h)
+
+        def park(m, h):
+            if h == 0:
+                result = result_pool.tile([P, H], F32, tag="result")
+                results[m] = result
+            nc.scalar.copy(out=results[m][:, h * N_PASS : (h + 1) * N_PASS], in_=own_acc[m][h][:])
+
+        def park_own_product(m):
+            open_own_product(m)
+            multiply_own(m)
+
+        def store(m, pieces=1):
+            width = H // pieces
+            for i in range(pieces):
+                cols = slice(i * width, (i + 1) * width)
                 nc.sync.dma_start(out=out[m * P : (m + 1) * P, cols], in_=results[m][:, cols])
 
         def multiply_mean(m):
@@ -230,8 +246,8 @@ def tile_graphsage_pa_kernel(
             for h in range(HALVES):
                 multiply(mean_acc[m], h, agg_x[m], agg_words, agg_plane, True, True)
 
-        def add_parked(m):
-            for h in range(HALVES):
+        def add_parked(m, halves=range(HALVES)):
+            for h in halves:
                 cols = slice(h * N_PASS, (h + 1) * N_PASS)
                 nc.vector.tensor_tensor(
                     out=results[m][:, cols],
@@ -255,14 +271,24 @@ def tile_graphsage_pa_kernel(
         sort_own(1)
         load_own(7)
         load_scale_rows(agg_plane, w1_0_scales)
-        agg_words = load_words("agg", w1_0_words)
+        agg_words = load_words("agg", w1_0_words, [slice(0, GROUPS)])
         for m in range(4):
             load_neigh(m)
         turn_own(0)
         turn_own(1)
         sort_own(2)
         sort_own(3)
-        for k in range(PARKED):
+        open_own_product(0)
+        open_own_product(1)
+        multiply_own(0, (0, 1))
+        multiply_own(1, (0, 1))
+        multiply_own(0, (2, 3))
+        turn_own(2)
+        turn_own(3)
+        multiply_own(1, (2, 3))
+        sort_own(4)
+        sort_own(5)
+        for k in range(2, PARKED):
             if k == 3:
                 sort_neigh(0, (0, 1))
             if k == 5:
@@ -299,14 +325,19 @@ def tile_graphsage_pa_kernel(
             if m > 2:
                 store(m - 3)
         add_parked(LAST - 1)
+        for h in range(HALVES):
+            cols = slice(h * N_PASS, (h + 1) * N_PASS)
+            rest = results[LAST - 1][:, cols]
+            nc.vector.tensor_scalar_max(rest, rest, 0.0)
         result = result_pool.tile([P, H], F32, tag="result")
         results[LAST] = result
-        relu(LAST - 1)
         for h in range(HALVES):
             cols = slice(h * N_PASS, (h + 1) * N_PASS)
             multiply(last_acc, h, agg_x[LAST], agg_words, agg_plane, False, True)
             nc.scalar.activation(
                 out=results[LAST][:, cols], in_=last_acc[h][:], func=mybir.ActivationFunctionType.Relu
             )
-        for m in range(LAST - 3, NODE_TILES):
+        for m in range(LAST - 3, LAST - 1):
             store(m)
+        store(LAST - 1, HALVES)
+        store(LAST, HALVES)

@@ -25,6 +25,8 @@ N_PASS = 512
 HALVES = H // N_PASS
 SCALE_ROWS = K_PASS // 32
 PARKED = 7
+FINE = 6
+LAST = NODE_TILES - 1
 OWN_PIECES = [slice(0, GROUPS // 2), slice(GROUPS // 2, GROUPS)]
 
 FLOPS = 2 * 2 * NODES * D * H + NODES * NEIGHBOURS * D
@@ -37,8 +39,8 @@ def tile_graphsage_pa_kernel(
     with ExitStack() as ctx:
         ctx.enter_context(tc.manual_schedule())
         const = ctx.enter_context(tc.tile_pool(name="const", bufs=1))
-        raw_own_pool = ctx.enter_context(tc.tile_pool(name="raw_own", bufs=6))
-        raw_neigh_pool = ctx.enter_context(tc.tile_pool(name="raw_neigh", bufs=4 * NEIGHBOURS))
+        raw_own_pool = ctx.enter_context(tc.tile_pool(name="raw_own", bufs=3))
+        raw_neigh_pool = ctx.enter_context(tc.tile_pool(name="raw_neigh", bufs=4 * NEIGHBOURS // 2))
         sorted_own_pool = ctx.enter_context(tc.tile_pool(name="sorted_own", bufs=4))
         sorted_neigh_pool = ctx.enter_context(
             tc.tile_pool(name="sorted_neigh", bufs=2 * NEIGHBOURS)
@@ -58,18 +60,31 @@ def tile_graphsage_pa_kernel(
         mean_acc = {}
         own_acc = {}
 
-        def load_own(m):
-            rows = raw_own_pool.tile([P, D], BF16, tag="raw_own")
-            nc.sync.dma_start(out=rows[:], in_=nf1[m * P : (m + 1) * P, :])
-            raw_own[m] = rows
+        def load_pair(rows, dram, first, at_once):
+            if at_once:
+                nc.sync.dma_start(
+                    out=rows[:],
+                    in_=dram[first : first + 2 * P, :].rearrange("(i p) d -> p i d", p=P),
+                )
+            else:
+                for i in range(2):
+                    nc.sync.dma_start(
+                        out=rows[:, i, :], in_=dram[first + i * P : first + (i + 1) * P, :]
+                    )
+
+        def load_own_pair(m, at_once):
+            rows = raw_own_pool.tile([P, 2, D], BF16, tag="raw_own")
+            load_pair(rows, nf1, m * P, at_once)
+            for i in range(2):
+                raw_own[m + i] = rows[:, i, :]
 
         def load_neigh(m):
             raw_neigh[m] = []
-            for a in range(NEIGHBOURS):
-                rows = raw_neigh_pool.tile([P, D], BF16, tag="raw_neigh")
-                first = (m * NEIGHBOURS + a) * P
-                nc.sync.dma_start(out=rows[:], in_=nf2[first : first + P, :])
-                raw_neigh[m].append(rows)
+            for a in range(0, NEIGHBOURS, 2):
+                rows = raw_neigh_pool.tile([P, 2, D], BF16, tag="raw_neigh")
+                load_pair(rows, nf2, (m * NEIGHBOURS + a) * P, m < FINE)
+                for i in range(2):
+                    raw_neigh[m].append(rows[:, i, :])
 
         def zero_plane(label):
             plane = const.tile([P, GROUPS, H], U8, name="plane_" + label, align_bytes=256)
@@ -92,13 +107,12 @@ def tile_graphsage_pa_kernel(
                 )
             return words
 
-        load_own(0)
-        load_own(1)
+        load_own_pair(0, False)
         own_plane = zero_plane("own")
         load_scale_rows(own_plane, w2_0_scales)
         own_words = load_words("own", w2_0_words, OWN_PIECES)
-        for m in range(2, 6):
-            load_own(m)
+        for m in range(2, 6, 2):
+            load_own_pair(m, True)
         agg_plane = zero_plane("agg")
 
         ident = const.tile([P, P], F32, name="ident")
@@ -117,14 +131,14 @@ def tile_graphsage_pa_kernel(
             ordered = pool.tile([P, D], BF16, tag=tag)
             copy(
                 out=ordered[:].bitcast(F32).rearrange("p (g u c i) -> p g c u i", g=GROUPS, u=2, i=4),
-                in_=raw[:].bitcast(F32).rearrange("p (g c i u) -> p g c u i", g=GROUPS, u=2, i=4),
+                in_=raw.bitcast(F32).rearrange("p (g c i u) -> p g c u i", g=GROUPS, u=2, i=4),
             )
             return ordered
 
         def sort_neigh(m, blocks=range(NEIGHBOURS)):
             for a in blocks:
                 if a == 3 and m >= 1:
-                    by_t = raw_neigh[m][a][:].rearrange(
+                    by_t = raw_neigh[m][a].rearrange(
                         "p (g c u e) -> p g u c e", g=GROUPS, u=2, e=2
                     )
                 else:
@@ -202,18 +216,22 @@ def tile_graphsage_pa_kernel(
                 banks.append(bank)
             return banks
 
-        def multiply(acc, h, x, w_words, w_plane, first, last, groups=range(GROUPS)):
+        def multiply_columns(bank, cols, x, w_words, w_plane, first, last, groups=range(GROUPS)):
             codes, scales = x
             for g in groups:
                 nc.tensor.matmul_mx(
-                    out=acc[h][:],
+                    out=bank[:],
                     lhsT=codes[:, g, :].bitcast(FP8X4),
                     lhsT_scale=scales[:, g, :],
-                    rhs=w_words[:, g, 2 * N_PASS * h : 2 * N_PASS * (h + 1)].bitcast(FP4X4),
-                    rhs_scale=w_plane[:, g, N_PASS * h : N_PASS * (h + 1)],
+                    rhs=w_words[:, g, 2 * cols.start : 2 * cols.stop].bitcast(FP4X4),
+                    rhs_scale=w_plane[:, g, cols],
                     start=first and g == 0,
                     stop=last and g == GROUPS - 1,
                 )
+
+        def multiply(acc, h, x, w_words, w_plane, first, last, groups=range(GROUPS)):
+            cols = slice(h * N_PASS, (h + 1) * N_PASS)
+            multiply_columns(acc[h], cols, x, w_words, w_plane, first, last, groups)
 
         def open_own_product(m):
             banks = new_acc(m % 2)
@@ -265,11 +283,18 @@ def tile_graphsage_pa_kernel(
                     func=mybir.ActivationFunctionType.Relu,
                 )
 
-        LAST = NODE_TILES - 1
+        def finish_columns(h, first, width):
+            cols = slice(h * N_PASS + first, h * N_PASS + first + width)
+            nc.scalar.activation(
+                out=results[LAST][:, cols],
+                in_=last_acc[h][:, first : first + width],
+                func=mybir.ActivationFunctionType.Relu,
+            )
+            nc.sync.dma_start(out=out[LAST * P : NODES, cols], in_=results[LAST][:, cols])
+
         sort_own(0)
-        load_own(6)
         sort_own(1)
-        load_own(7)
+        load_own_pair(6, True)
         load_scale_rows(agg_plane, w1_0_scales)
         agg_words = load_words("agg", w1_0_words, [slice(0, GROUPS)])
         for m in range(4):
@@ -313,10 +338,11 @@ def tile_graphsage_pa_kernel(
                 add_parked(m - 1)
             grouped = turn_mean(m + 1)
             if m + 2 < NODE_TILES:
-                sort_neigh(m + 2, (0, 1, 2))
+                early = range(2 if m + 2 == LAST else 3)
+                sort_neigh(m + 2, early)
             quantise_mean(m + 1, grouped)
             if m + 2 < NODE_TILES:
-                sort_neigh(m + 2, (3,))
+                sort_neigh(m + 2, range(len(early), NEIGHBOURS))
             if m + 5 < NODE_TILES:
                 load_neigh(m + 5)
             multiply_mean(m)
@@ -331,13 +357,12 @@ def tile_graphsage_pa_kernel(
             nc.vector.tensor_scalar_max(rest, rest, 0.0)
         result = result_pool.tile([P, H], F32, tag="result")
         results[LAST] = result
-        for h in range(HALVES):
-            cols = slice(h * N_PASS, (h + 1) * N_PASS)
-            multiply(last_acc, h, agg_x[LAST], agg_words, agg_plane, False, True)
-            nc.scalar.activation(
-                out=results[LAST][:, cols], in_=last_acc[h][:], func=mybir.ActivationFunctionType.Relu
-            )
         for m in range(LAST - 3, LAST - 1):
             store(m)
         store(LAST - 1, HALVES)
-        store(LAST, HALVES)
+        for h, widths in enumerate(((512,), (512,))):
+            multiply(last_acc, h, agg_x[LAST], agg_words, agg_plane, False, True)
+            first = 0
+            for width in widths:
+                finish_columns(h, first, width)
+                first += width

@@ -91,8 +91,8 @@ def tile_graphsage_pa_kernel(
             nc.vector.memset(plane[:].bitcast(I32), 0)
             return plane
 
-        def load_scale_rows(plane, scales_dram):
-            for r in range(4):
+        def load_scale_rows(plane, scales_dram, rows=range(4)):
+            for r in rows:
                 nc.sync.dma_start(
                     out=plane[r:P:32, :, :].bitcast(I32),
                     in_=scales_dram.bitcast(I32)[:, r:SCALE_ROWS:4, :].rearrange("g q n -> q g n"),
@@ -295,10 +295,15 @@ def tile_graphsage_pa_kernel(
         sort_own(0)
         sort_own(1)
         load_own_pair(6, True)
-        load_scale_rows(agg_plane, w1_0_scales)
+        load_scale_rows(agg_plane, w1_0_scales, (0,))
+        load_neigh(0)
+        load_scale_rows(agg_plane, w1_0_scales, (1,))
         agg_words = load_words("agg", w1_0_words, [slice(0, GROUPS)])
-        for m in range(4):
-            load_neigh(m)
+        load_scale_rows(agg_plane, w1_0_scales, (2,))
+        load_neigh(1)
+        load_scale_rows(agg_plane, w1_0_scales, (3,))
+        load_neigh(2)
+        load_neigh(3)
         turn_own(0)
         turn_own(1)
         sort_own(2)

from contextlib import ExitStack

import concourse.mybir as mybir
from concourse.masks import make_identity

BF16 = mybir.dt.bfloat16
F32 = mybir.dt.float32
I32 = mybir.dt.int32
U8 = mybir.dt.uint8
U32 = mybir.dt.uint32
FP8X4 = mybir.dt.float8_e4m3fn_x4
FP4X4 = mybir.dt.float4_e2m1fn_x4

P = 128
PACK = 4
K_PASS = P * PACK
NODES = 1024
NEIGHBOURS = 4
D = 2048
H = 1024
GROUPS = D // K_PASS
NODE_TILES = NODES // P
NODES_PER_LOAD = P // NEIGHBOURS
N_PASS = 512
HALVES = H // N_PASS
SCALE_ROWS = K_PASS // 32
PARKED = 7
FINE = 6
LAST = NODE_TILES - 1
OWN_PIECES = [slice(0, GROUPS // 2), slice(GROUPS // 2, GROUPS)]

FLOPS = 2 * 2 * NODES * D * H + NODES * NEIGHBOURS * D


def tile_graphsage_pa_kernel(
    tc, nf1, nf2, w1_0_words, w1_0_scales, w2_0_words, w2_0_scales, out
):
    nc = tc.nc
    with ExitStack() as ctx:
        ctx.enter_context(tc.manual_schedule())
        const = ctx.enter_context(tc.tile_pool(name="const", bufs=1))
        raw_own_pool = ctx.enter_context(tc.tile_pool(name="raw_own", bufs=3))
        raw_neigh_pool = ctx.enter_context(tc.tile_pool(name="raw_neigh", bufs=4 * NEIGHBOURS // 2))
        sorted_own_pool = ctx.enter_context(tc.tile_pool(name="sorted_own", bufs=4))
        sorted_neigh_pool = ctx.enter_context(
            tc.tile_pool(name="sorted_neigh", bufs=2 * NEIGHBOURS)
        )
        work = ctx.enter_context(tc.tile_pool(name="work", bufs=2))
        own_ops = ctx.enter_context(tc.tile_pool(name="own_ops", bufs=4))
        result_pool = ctx.enter_context(tc.tile_pool(name="result", bufs=NODE_TILES))
        psum = ctx.enter_context(tc.psum_pool(name="psum", bufs=1))

        raw_own = {}
        raw_neigh = {}
        sorted_own = {}
        sorted_neigh = {}
        own_x = {}
        agg_x = {}
        results = {}
        mean_acc = {}
        own_acc = {}

        def load_pair(rows, dram, first, at_once):
            if at_once:
                nc.sync.dma_start(
                    out=rows[:],
                    in_=dram[first : first + 2 * P, :].rearrange("(i p) d -> p i d", p=P),
                )
            else:
                for i in range(2):
                    nc.sync.dma_start(
                        out=rows[:, i, :], in_=dram[first + i * P : first + (i + 1) * P, :]
                    )

        def load_own_pair(m, at_once):
            rows = raw_own_pool.tile([P, 2, D], BF16, tag="raw_own")
            load_pair(rows, nf1, m * P, at_once)
            for i in range(2):
                raw_own[m + i] = rows[:, i, :]

        def load_neigh(m):
            raw_neigh[m] = []
            for a in range(0, NEIGHBOURS, 2):
                rows = raw_neigh_pool.tile([P, 2, D], BF16, tag="raw_neigh")
                load_pair(rows, nf2, (m * NEIGHBOURS + a) * P, m < FINE)
                for i in range(2):
                    raw_neigh[m].append(rows[:, i, :])

        def zero_plane(label):
            plane = const.tile([P, GROUPS, H], U8, name="plane_" + label, align_bytes=256)
            nc.vector.memset(plane[:].bitcast(I32), 0)
            return plane

        def load_scale_rows(plane, scales_dram, rows=range(4)):
            for r in rows:
                nc.sync.dma_start(
                    out=plane[r:P:32, :, :].bitcast(I32),
                    in_=scales_dram.bitcast(I32)[:, r:SCALE_ROWS:4, :].rearrange("g q n -> q g n"),
                )

        def load_words(label, words_dram, pieces):
            words = const.tile([P, GROUPS, 2 * H], U8, name="words_" + label, align_bytes=256)
            for groups in pieces:
                nc.sync.dma_start(
                    out=words[:, groups, :].bitcast(I32),
                    in_=words_dram.bitcast(I32)[groups, :, :].rearrange("g p b -> p g b"),
                )
            return words

        load_own_pair(0, False)
        own_plane = zero_plane("own")
        load_scale_rows(own_plane, w2_0_scales)
        own_words = load_words("own", w2_0_words, OWN_PIECES)
        for m in range(2, 6, 2):
            load_own_pair(m, True)
        agg_plane = zero_plane("agg")

        ident = const.tile([P, P], F32, name="ident")
        make_identity(nc, ident[:])
        group_of_row = const.tile([P, NODES_PER_LOAD], F32, name="group_of_row")
        nc.vector.tensor_reduce(
            out=group_of_row[:],
            in_=ident[:].rearrange("p (n j) -> p n j", j=NEIGHBOURS),
            axis=mybir.AxisListType.X,
            op=mybir.AluOpType.add,
        )
        mean_weights = const.tile([P, NODES_PER_LOAD], BF16, name="mean_weights")
        nc.vector.tensor_scalar_mul(mean_weights[:], group_of_row[:], 1.0 / NEIGHBOURS)

        def sort_words(copy, pool, tag, raw):
            ordered = pool.tile([P, D], BF16, tag=tag)
            copy(
                out=ordered[:].bitcast(F32).rearrange("p (g u c i) -> p g c u i", g=GROUPS, u=2, i=4),
                in_=raw.bitcast(F32).rearrange("p (g c i u) -> p g c u i", g=GROUPS, u=2, i=4),
            )
            return ordered

        def sort_neigh(m, blocks=range(NEIGHBOURS)):
            for a in blocks:
                if a == 3 and m >= 1:
                    by_t = raw_neigh[m][a].rearrange(
                        "p (g c u e) -> p g u c e", g=GROUPS, u=2, e=2
                    )
                else:
                    ordered = sort_words(
                        nc.vector.tensor_copy, sorted_neigh_pool, "sorted_neigh", raw_neigh[m][a]
                    )
                    by_t = ordered[:].rearrange("p (g u c e) -> p g u c e", g=GROUPS, u=2, e=2)
                sorted_neigh.setdefault(m, []).append(by_t)

        def quantise(pool, label, grouped):
            codes = pool.tile([P, GROUPS, P], U32, tag="codes_" + label, align_bytes=256)
            scales = pool.tile([P, GROUPS, P], U8, tag="scales_" + label, align_bytes=256)
            nc.vector.quantize_mx(
                out=codes[:].rearrange("p g n -> p (g n)").bitcast(FP8X4),
                scales=scales[:].rearrange("p g n -> p (g n)"),
                in_=grouped[:].rearrange("p g n t -> p (g n t)"),
            )
            return codes, scales

        def sort_own(m):
            sorted_own[m] = sort_words(
                nc.vector.tensor_copy, sorted_own_pool, "sorted_own", raw_own[m]
            )

        def turn_own(m):
            words = sorted_own[m][:].bitcast(F32)
            grouped = work.tile([P, GROUPS, P, PACK], BF16, tag="grouped_own", align_bytes=256)
            for pair in range(GROUPS // 2):
                turned = psum.tile([P, 2, 2, P], F32, tag="turn%d" % (2 * (m % 2) + pair))
                for i in range(2):
                    for u in range(2):
                        first = ((2 * pair + i) * 2 + u) * P
                        nc.tensor.transpose(
                            out=turned[:, i, u, :],
                            in_=words[:, first : first + P],
                            identity=ident[:],
                        )
                copy = nc.scalar.copy if pair == 0 else nc.vector.tensor_copy
                copy(
                    out=grouped[:, 2 * pair : 2 * pair + 2, :, :].bitcast(F32),
                    in_=turned[:].rearrange("p i u n -> p i n u"),
                )
            own_x[m] = quantise(own_ops, "own", grouped)

        def turn_mean(m):
            grouped = work.tile([P, GROUPS, P, PACK], BF16, tag="grouped_agg", align_bytes=256)
            turned = []
            for g in range(GROUPS):
                bank = psum.tile([P, PACK, P], F32, tag="turn%d" % g)
                turned.append(bank)
            order = [(a, g) for g in range(GROUPS) for a in range(NEIGHBOURS)] if m != 7 else [(a, g) for a in range(NEIGHBOURS) for g in range(GROUPS)]
            for a, g in order:
                nodes = slice(a * NODES_PER_LOAD, (a + 1) * NODES_PER_LOAD)
                by_t = sorted_neigh[m][a]
                for t in range(PACK):
                    nc.tensor.matmul(
                        out=turned[g][:, t, nodes],
                        lhsT=by_t[:, g, t // 2, :, t % 2],
                        rhs=mean_weights[:],
                        start=True,
                        stop=True,
                    )
            for g in range(GROUPS):
                copy = nc.vector.tensor_copy if (m in (0, 7) and g % 2 == 1) else nc.scalar.copy
                copy(out=grouped[:, g, :, :], in_=turned[g][:].rearrange("p t n -> p n t"))
            return grouped

        def quantise_mean(m, grouped):
            agg_x[m] = quantise(work, "agg", grouped)

        def new_acc(s):
            banks = []
            for h in range(HALVES):
                bank = psum.tile([P, N_PASS], F32, tag="acc%d" % (2 * s + h))
                banks.append(bank)
            return banks

        def multiply_columns(bank, cols, x, w_words, w_plane, first, last, groups=range(GROUPS)):
            codes, scales = x
            for g in groups:
                nc.tensor.matmul_mx(
                    out=bank[:],
                    lhsT=codes[:, g, :].bitcast(FP8X4),
                    lhsT_scale=scales[:, g, :],
                    rhs=w_words[:, g, 2 * cols.start : 2 * cols.stop].bitcast(FP4X4),
                    rhs_scale=w_plane[:, g, cols],
                    start=first and g == 0,
                    stop=last and g == GROUPS - 1,
                )

        def multiply(acc, h, x, w_words, w_plane, first, last, groups=range(GROUPS)):
            cols = slice(h * N_PASS, (h + 1) * N_PASS)
            multiply_columns(acc[h], cols, x, w_words, w_plane, first, last, groups)

        def open_own_product(m):
            banks = new_acc(m % 2)
            own_acc[m] = banks

        def multiply_own(m, groups=range(GROUPS)):
            for h in range(HALVES):
                multiply(own_acc[m], h, own_x[m], own_words, own_plane, True, True, groups)
                if GROUPS - 1 in groups:
                    park(m, h)

        def park(m, h):
            if h == 0:
                result = result_pool.tile([P, H], F32, tag="result")
                results[m] = result
            nc.scalar.copy(out=results[m][:, h * N_PASS : (h + 1) * N_PASS], in_=own_acc[m][h][:])

        def park_own_product(m):
            open_own_product(m)
            multiply_own(m)

        def store(m, pieces=1):
            width = H // pieces
            for i in range(pieces):
                cols = slice(i * width, (i + 1) * width)
                nc.sync.dma_start(out=out[m * P : (m + 1) * P, cols], in_=results[m][:, cols])

        def multiply_mean(m):
            mean_acc[m] = new_acc(0)
            for h in range(HALVES):
                multiply(mean_acc[m], h, agg_x[m], agg_words, agg_plane, True, True)

        def add_parked(m, halves=range(HALVES)):
            for h in halves:
                cols = slice(h * N_PASS, (h + 1) * N_PASS)
                nc.vector.tensor_tensor(
                    out=results[m][:, cols],
                    in0=mean_acc[m][h][:],
                    in1=results[m][:, cols],
                    op=mybir.AluOpType.add,
                )

        def relu(m):
            for h in range(HALVES):
                cols = slice(h * N_PASS, (h + 1) * N_PASS)
                nc.scalar.activation(
                    out=results[m][:, cols],
                    in_=results[m][:, cols],
                    func=mybir.ActivationFunctionType.Relu,
                )

        def finish_columns(h, first, width):
            cols = slice(h * N_PASS + first, h * N_PASS + first + width)
            nc.scalar.activation(
                out=results[LAST][:, cols],
                in_=last_acc[h][:, first : first + width],
                func=mybir.ActivationFunctionType.Relu,
            )
            nc.sync.dma_start(out=out[LAST * P : NODES, cols], in_=results[LAST][:, cols])

        sort_own(0)
        sort_own(1)
        load_own_pair(6, True)
        load_scale_rows(agg_plane, w1_0_scales, (0,))
        load_neigh(0)
        load_scale_rows(agg_plane, w1_0_scales, (1,))
        agg_words = load_words("agg", w1_0_words, [slice(0, GROUPS)])
        load_scale_rows(agg_plane, w1_0_scales, (2,))
        load_neigh(1)
        load_scale_rows(agg_plane, w1_0_scales, (3,))
        load_neigh(2)
        load_neigh(3)
        turn_own(0)
        turn_own(1)
        sort_own(2)
        sort_own(3)
        open_own_product(0)
        open_own_product(1)
        multiply_own(0, (0, 1))
        multiply_own(1, (0, 1))
        multiply_own(0, (2, 3))
        turn_own(2)
        turn_own(3)
        multiply_own(1, (2, 3))
        sort_own(4)
        sort_own(5)
        for k in range(2, PARKED):
            if k == 3:
                sort_neigh(0, (0, 1))
            if k == 5:
                sort_neigh(0, (2, 3))
                sort_neigh(1, (0, 1))
            park_own_product(k)
            if k % 2 == 0 and k + 2 < NODE_TILES:
                turn_own(k + 2)
                turn_own(k + 3)
                if k + 4 < NODE_TILES:
                    sort_own(k + 4)
                    sort_own(k + 5)
        grouped = turn_mean(0)
        quantise_mean(0, grouped)
        sort_neigh(1, (2, 3))
        load_neigh(4)
        last_acc = new_acc(1)
        for h in range(HALVES):
            multiply(last_acc, h, own_x[LAST], own_words, own_plane, True, False)
        for m in range(LAST):
            if m > 0:
                add_parked(m - 1)
            grouped = turn_mean(m + 1)
            if m + 2 < NODE_TILES:
                early = range(2 if m + 2 == LAST else 3)
                sort_neigh(m + 2, early)
            quantise_mean(m + 1, grouped)
            if m + 2 < NODE_TILES:
                sort_neigh(m + 2, range(len(early), NEIGHBOURS))
            if m + 5 < NODE_TILES:
                load_neigh(m + 5)
            multiply_mean(m)
            if m > 0:
                relu(m - 1)
            if m > 2:
                store(m - 3)
        add_parked(LAST - 1)
        for h in range(HALVES):
            cols = slice(h * N_PASS, (h + 1) * N_PASS)
            rest = results[LAST - 1][:, cols]
            nc.vector.tensor_scalar_max(rest, rest, 0.0)
        result = result_pool.tile([P, H], F32, tag="result")
        results[LAST] = result
        for m in range(LAST - 3, LAST - 1):
            store(m)
        store(LAST - 1, HALVES)
        for h, widths in enumerate(((512,), (512,))):
            multiply(last_acc, h, agg_x[LAST], agg_words, agg_plane, False, True)
            first = 0
            for width in widths:
                finish_columns(h, first, width)
                first += width
